import numpy as np
import ml_dtypes


def mxq(x, axis, fmt="e4m3"):
    dtype, down = {"e4m3": (ml_dtypes.float8_e4m3fn, 7), "e5m2": (ml_dtypes.float8_e5m2, 14)}[fmt]
    v = np.moveaxis(np.asarray(x, np.float32).astype(ml_dtypes.bfloat16).astype(np.float64), axis, -1)
    blocks = v.reshape(v.shape[:-1] + (-1, 32))
    amax = np.abs(blocks).max(-1, keepdims=True)
    byte = np.maximum(np.where(amax > 0, np.frexp(amax)[1] - 1 + 127, 0) - down, 1)
    scale = np.exp2(byte - 127.0)
    codes = (blocks / scale).astype(np.float32).astype(dtype).astype(np.float64)
    return np.moveaxis((codes * scale).reshape(v.shape), -1, axis)


WIDE = False


def mx_kscale(k):
    if not WIDE:
        return np.ones(k)
    levels = np.array([10, -10, 5, -5, 0])
    a = np.random.permutation(np.resize(levels, k // 512 * 4)).reshape(k // 512, 4)
    idx = np.arange(k)
    return np.exp2(a[idx // 512, idx % 128 // 32])


BF16 = ml_dtypes.bfloat16


def bf(x):
    return np.asarray(x, np.float32).astype(BF16)


def f64(x):
    return np.asarray(x).astype(np.float64)


B, K, H, D = 128, 128, 512, 64
C = 0.2
HALF_LOG_2PI = 0.5 * np.log(2.0 * np.pi)


def log_softmax(v, axis):
    v = v - v.max(axis=axis, keepdims=True)
    return v - np.log(np.exp(v).sum(axis=axis, keepdims=True))


def logsumexp(v, axis):
    m = v.max(axis=axis, keepdims=True)
    return np.log(np.exp(v - m).sum(axis=axis)) + np.squeeze(m, axis)


def contract(xq, vq):
    return (xq.transpose(2, 0, 1) @ vq.transpose(2, 1, 0)).transpose(1, 2, 0)


def setup_inputs():
    s = mx_kscale(H)[None, :, None]
    r = 1.0 / np.sqrt(H)
    return {
        "x": bf(np.random.standard_normal((B, H, D)) * s),
        "input_var": bf(np.random.standard_normal((B, D)) * C),
        "V_alpha": bf(np.random.standard_normal((K, H, D)) * r / s),
        "V_mu": bf(np.random.standard_normal((K, H, D)) * C * r / s),
        "V_sigma": bf(np.random.standard_normal((K, H, D)) * 0.5 * r / s),
        "b_alpha": bf(np.random.standard_normal((K, D)) * 0.7),
        "b_mu": bf(np.random.standard_normal((K, D)) * 0.5 * C),
        "b_sigma": bf(np.log(C) + np.random.standard_normal((K, D)) * 0.3),
    }


def reference(x, input_var, V_alpha, V_mu, V_sigma, b_alpha, b_mu, b_sigma):
    xq = mxq(f64(x), 1, "e4m3")
    exp_alpha = contract(xq, mxq(f64(V_alpha), 1, "e4m3")) + f64(b_alpha)
    log_alpha = log_softmax(exp_alpha, 1)
    mu = contract(xq, mxq(f64(V_mu), 1, "e4m3")) + f64(b_mu)
    log_sigma = np.clip(contract(xq, mxq(f64(V_sigma), 1, "e4m3")) + f64(b_sigma), -20.0, 20.0)
    sigma = np.exp(log_sigma)
    y = f64(input_var)[:, None, :]
    log_p = -0.5 * np.square((y - mu) / sigma) + log_alpha - HALF_LOG_2PI - log_sigma
    return np.sum(logsumexp(log_p, 1), axis=1)

@@ -1,0 +1,370 @@
+import math
+
+import concourse.mybir as mybir
+from concourse.masks import make_identity
+
+BF16 = mybir.dt.bfloat16
+F32 = mybir.dt.float32
+U32 = mybir.dt.uint32
+U8 = mybir.dt.uint8
+FP8X4 = mybir.dt.float8_e4m3fn_x4
+ALU = mybir.AluOpType
+ACT = mybir.ActivationFunctionType
+AX = mybir.AxisListType
+
+P = 128
+ROWS = 128
+H = 512
+D = 64
+PACK = 4
+HALF = 64
+CHUNK = 8
+RUN = 4
+D_VECTOR_FIRST = 32
+D_VECTOR_LATER = 40
+GROUP = 4
+N_GROUPS = D // GROUP
+Y_BANK = 8
+EVERY_VECTOR = 17
+LAG = 2
+HALF_LOG_2PI = 0.5 * math.log(2.0 * math.pi)
+
+FLOPS = 2 * ROWS * ROWS * H * D * 3
+
+
+def load_and_quantise(
+    nc, raw_pool, grouped_tiles, d_vector, src, codes, scales, other_work=None, leave_last_half=False,
+    small_start=False,
+):
+    by_partition = src.rearrange("r (p j) d -> p r (j d)", j=PACK)
+    for half in range(ROWS // HALF):
+        grouped = grouped_tiles[half % len(grouped_tiles)]
+        sizes = [CHUNK] * (HALF // CHUNK)
+        if small_start and half == 0:
+            sizes = [CHUNK // 4, CHUNK // 4, CHUNK // 2] + sizes[1:]
+        row_in_half = 0
+        for size in sizes:
+            first_row = half * HALF + row_in_half
+            raw = raw_pool.tile([P, size, PACK * D], BF16, tag="raw")
+            nc.sync.dma_start(out=raw[:], in_=by_partition[:, first_row : first_row + size, :])
+            raw_mj = raw[:].rearrange("p r (j d) -> p (r j) d", j=PACK)
+            cols = slice(row_in_half * PACK, (row_in_half + size) * PACK)
+            row_in_half += size
+            for copy, d_range in (
+                (nc.vector.tensor_copy, slice(0, d_vector)),
+                (nc.scalar.copy, slice(d_vector, D)),
+            ):
+                copy(
+                    out=grouped[:, d_range, cols].rearrange("p (c i) m -> p c m i", i=RUN),
+                    in_=raw_mj[:, :, d_range].rearrange("p m (c i) -> p c m i", i=RUN),
+                )
+            if other_work is not None:
+                other_work(first_row // CHUNK)
+        if leave_last_half and half == ROWS // HALF - 1:
+            break
+        rows = slice(half * HALF, (half + 1) * HALF)
+        for d in range(D):
+            nc.vector.quantize_mx(
+                out=codes[:, d, rows].bitcast(FP8X4),
+                scales=scales[:, d, rows],
+                in_=grouped[:, d, :],
+            )
+
+
+def tile_rnadeoutputlayer_kernel(
+    tc, x, input_var, V_alpha, V_mu, V_sigma, b_alpha, b_mu, b_sigma, out
+):
+    nc = tc.nc
+    with (
+        tc.tile_pool(name="keep", bufs=1) as keep,
+        tc.tile_pool(name="raw", bufs=7) as raw_pool,
+        tc.tile_pool(name="work", bufs=2) as work,
+        tc.psum_pool(name="acc", bufs=4) as psum_acc,
+        tc.psum_pool(name="tp", bufs=3) as psum_tp,
+        tc.psum_pool(name="spare", bufs=1) as psum_spare,
+    ):
+        ident = keep.tile([P, P], F32)
+        make_identity(nc, ident[:])
+        ident_bf = keep.tile([P, P], BF16)
+        make_identity(nc, ident_bf[:])
+
+        y_bf = keep.tile([P, D], BF16)
+        nc.scalar.dma_start(out=y_bf[:], in_=input_var)
+        bias_bf = keep.tile([P, 3, D], BF16)
+        nc.scalar.dma_start(out=bias_bf[:, 0, :], in_=b_sigma)
+        nc.scalar.dma_start(out=bias_bf[:, 1, :], in_=b_mu)
+        nc.scalar.dma_start(out=bias_bf[:, 2, :], in_=b_alpha)
+        bias_sigma = keep.tile([P, D], F32)
+        bias_mu = keep.tile([P, D], F32)
+        neg_bias_alpha = keep.tile([P, D], F32)
+        nc.vector.tensor_copy(out=bias_sigma[:], in_=bias_bf[:, 0, :])
+        nc.vector.tensor_copy(out=bias_mu[:], in_=bias_bf[:, 1, :])
+        nc.vector.tensor_scalar(
+            out=neg_bias_alpha[:], in0=bias_bf[:, 2, :], scalar1=-1.0, scalar2=None, op0=ALU.mult
+        )
+
+        grouped = keep.tile([P, D, HALF * PACK], BF16, align_bytes=64)
+        x_codes = keep.tile([P, D, ROWS], U32, align_bytes=64)
+        x_scales = keep.tile([P, D, ROWS], U8, align_bytes=64)
+        w_codes = keep.tile([P, D, ROWS], U32, align_bytes=64)
+        w_scales = keep.tile([P, D, ROWS], U8, align_bytes=64)
+        neg_a = keep.tile([P, D, ROWS], F32)
+        y_all = keep.tile([P, D, ROWS], BF16)
+        neg_max = keep.tile([P, 2, D], F32)
+        exp_sum = keep.tile([P, 2, D], F32)
+
+        def products(g):
+            acc = psum_acc.tile([P, GROUP, ROWS], F32, tag="acc")
+            for i in range(GROUP):
+                d = g * GROUP + i
+                nc.tensor.matmul_mx(
+                    out=acc[:, i, :],
+                    lhsT=w_codes[:, d, :].bitcast(FP8X4),
+                    lhsT_scale=w_scales[:, d, :],
+                    rhs=x_codes[:, d, :].bitcast(FP8X4),
+                    rhs_scale=x_scales[:, d, :],
+                    start=True,
+                    stop=True,
+                )
+            return acc
+
+        def turn(terms_of):
+            by_b = psum_tp.tile([P, GROUP, ROWS], F32, tag="tp")
+            for i in range(GROUP):
+                terms = terms_of(i)
+                for t, term in enumerate(terms):
+                    nc.tensor.matmul(
+                        out=by_b[:, i, :],
+                        lhsT=term,
+                        rhs=ident[:],
+                        is_transpose=True,
+                        start=(t == 0),
+                        stop=(t == len(terms) - 1),
+                    )
+            return by_b
+
+        def max_and_sum(g, w, by_b):
+            ds = slice(g * GROUP, (g + 1) * GROUP)
+            nc.vector.tensor_reduce(out=neg_max[:, w, ds], in_=by_b[:], axis=AX.X, op=ALU.min)
+            unused = work.tile([P, GROUP, ROWS], BF16, tag="unused")
+            for i in range(GROUP):
+                d = g * GROUP + i
+                nc.scalar.activation(
+                    out=unused[:, i, :],
+                    in_=by_b[:, i, :],
+                    func=ACT.Exp,
+                    bias=neg_max[:, w, d : d + 1],
+                    scale=-1.0,
+                    accum_out=exp_sum[:, w, d : d + 1],
+                )
+
+        def reduce_over_k(g, w, terms_of):
+            max_and_sum(g, w, turn(terms_of))
+
+        for first in range(0, D, Y_BANK):
+            spread = psum_acc.tile([P, Y_BANK, ROWS], BF16, tag="acc")
+            for i in range(Y_BANK):
+                d = first + i
+                nc.tensor.matmul(
+                    out=spread[:, i, :],
+                    lhsT=y_bf[:, d : d + 1].to_broadcast([P, P]),
+                    rhs=ident_bf[:],
+                    start=True,
+                    stop=True,
+                )
+            nc.vector.tensor_copy(out=y_all[:, first : first + Y_BANK, :], in_=spread[:])
+
+        with tc.tile_pool(name="early", bufs=1) as early:
+            grouped_too = early.tile([P, D, HALF * PACK], BF16, align_bytes=64)
+            two_grouped = [grouped, grouped_too]
+
+            load_and_quantise(
+                nc, raw_pool, two_grouped, D_VECTOR_FIRST, x, x_codes, x_scales, None, False, True
+            )
+            load_and_quantise(
+                nc, raw_pool, two_grouped, D_VECTOR_FIRST, V_alpha, w_codes, w_scales
+            )
+
+            for g in range(N_GROUPS):
+                acc = products(g)
+                for i in range(GROUP):
+                    d = g * GROUP + i
+                    if g % EVERY_VECTOR != EVERY_VECTOR - 1:
+                        nc.scalar.activation(
+                            out=neg_a[:, d, :],
+                            in_=acc[:, i, :],
+                            func=ACT.Identity,
+                            bias=neg_bias_alpha[:, d : d + 1],
+                            scale=-1.0,
+                        )
+                    else:
+                        nc.vector.tensor_scalar(
+                            out=neg_a[:, d, :],
+                            in0=acc[:, i, :],
+                            scalar1=-1.0,
+                            scalar2=neg_bias_alpha[:, d : d + 1],
+                            op0=ALU.mult,
+                            op1=ALU.add,
+                        )
+
+            def alpha_group(g):
+                reduce_over_k(g, 0, lambda i: [neg_a[:, g * GROUP + i, :]])
+
+            def alpha_first_half(step):
+                if step % 2 == 0:
+                    alpha_group(step // 2)
+
+            load_and_quantise(
+                nc, raw_pool, two_grouped, D_VECTOR_LATER, V_sigma, w_codes, w_scales, alpha_first_half
+            )
+
+        with tc.tile_pool(name="late", bufs=1) as late:
+            log_sigma = late.tile([P, D, ROWS], F32)
+
+            spare = psum_spare.tile([P, GROUP * ROWS], F32)
+            half_z2_of = {}
+            inv_sigma_of = {}
+
+            acc_of = {}
+            by_b_of = {}
+
+            def extra_pass():
+                nc.tensor.matmul_mx(
+                    out=spare[:],
+                    lhsT=x_codes[:, 0, :].bitcast(FP8X4),
+                    lhsT_scale=x_scales[:, 0, :],
+                    rhs=x_codes[:, 0:GROUP, :].rearrange("p d r -> p (d r)").bitcast(FP8X4),
+                    rhs_scale=x_scales[:, 0:GROUP, :].rearrange("p d r -> p (d r)"),
+                    start=True,
+                    stop=True,
+                )
+
+            def quantise_rest(g):
+                for d in range(g * GROUP, (g + 1) * GROUP):
+                    nc.vector.quantize_mx(
+                        out=w_codes[:, d, HALF:ROWS].bitcast(FP8X4),
+                        scales=w_scales[:, d, HALF:ROWS],
+                        in_=grouped[:, d, :],
+                    )
+
+            def passes(g):
+                ds = slice(g * GROUP, (g + 1) * GROUP)
+                acc_of[g] = products(g)
+                extra_pass()
+                inv_sigma = work.tile([P, GROUP, ROWS], F32, tag="inv_sigma")
+                nc.scalar.activation(
+                    out=inv_sigma[:], in_=log_sigma[:, ds, :], func=ACT.Exp, scale=-1.0
+                )
+                inv_sigma_of[g] = inv_sigma
+
+            def difference(g):
+                acc = acc_of[g]
+                half_z2 = work.tile([P, GROUP, ROWS], F32, tag="half_z2", bufs=LAG + 1)
+                for i in range(GROUP):
+                    d = g * GROUP + i
+                    nc.vector.scalar_tensor_tensor(
+                        out=half_z2[:, i, :],
+                        in0=acc[:, i, :],
+                        scalar=bias_mu[:, d : d + 1],
+                        in1=y_all[:, d, :],
+                        op0=ALU.add,
+                        op1=ALU.subtract,
+                    )
+                half_z2_of[g] = half_z2
+
+            def scaled_square(g):
+                half_z2 = half_z2_of[g]
+                nc.vector.tensor_tensor(
+                    out=half_z2[:], in0=half_z2[:], in1=inv_sigma_of[g][:], op=ALU.mult
+                )
+                nc.scalar.activation(
+                    out=half_z2[:], in_=half_z2[:], func=ACT.Square, scale=math.sqrt(0.5)
+                )
+
+            def exponent(g):
+                by_b_of[g] = turn(
+                    lambda i: [
+                        neg_a[:, g * GROUP + i, :],
+                        log_sigma[:, g * GROUP + i, :],
+                        half_z2_of[g][:, i, :],
+                    ]
+                )
+
+            for g in range(N_GROUPS):
+                ds = slice(g * GROUP, (g + 1) * GROUP)
+                acc = products(g)
+                for i in range(GROUP):
+                    d = g * GROUP + i
+                    nc.scalar.activation(
+                        out=log_sigma[:, d, :],
+                        in_=acc[:, i, :],
+                        func=ACT.Identity,
+                        bias=bias_sigma[:, d : d + 1],
+                        scale=1.0,
+                    )
+                nc.vector.tensor_scalar(
+                    out=log_sigma[:, ds, :],
+                    in0=log_sigma[:, ds, :],
+                    scalar1=-20.0,
+                    scalar2=20.0,
+                    op0=ALU.max,
+                    op1=ALU.min,
+                )
+
+            def alpha_second_half(step):
+                if step % 2 == 0:
+                    alpha_group(N_GROUPS // 2 + step // 2)
+
+            load_and_quantise(
+                nc, raw_pool, [grouped], D_VECTOR_LATER, V_mu, w_codes, w_scales, alpha_second_half, True
+            )
+            with tc.manual_schedule(engines={mybir.EngineType.PE, mybir.EngineType.DVE}):
+                quantise_rest(0)
+                for s in range(N_GROUPS + LAG + 2):
+                    if s + 1 < N_GROUPS:
+                        quantise_rest(s + 1)
+                    if s < N_GROUPS:
+                        passes(s)
+                    if 1 <= s <= N_GROUPS:
+                        scaled_square(s - 1)
+                    if LAG <= s < N_GROUPS + LAG:
+                        exponent(s - LAG)
+                    if s == N_GROUPS:
+                        extra_pass()
+                        extra_pass()
+                    if s >= LAG + 1 and s - LAG - 1 < N_GROUPS:
+                        max_and_sum(s - LAG - 1, 1, by_b_of[s - LAG - 1])
+                    if s < N_GROUPS:
+                        difference(s)
+
+            log_sum = late.tile([P, 2, D], F32)
+            log_total = late.tile([P, 2], F32)
+            for w in range(2):
+                nc.scalar.activation(
+                    out=log_sum[:, w, :],
+                    in_=exp_sum[:, w, :],
+                    func=ACT.Ln,
+                    accum_out=log_total[:, w : w + 1],
+                )
+            neg_max_total = late.tile([P, 2], F32)
+            nc.vector.tensor_reduce(out=neg_max_total[:], in_=neg_max[:], axis=AX.X, op=ALU.add)
+            lse_total = late.tile([P, 2], F32)
+            nc.vector.tensor_tensor(
+                out=lse_total[:], in0=log_total[:], in1=neg_max_total[:], op=ALU.subtract
+            )
+            result = late.tile([P, 1], F32)
+            nc.vector.tensor_scalar(
+                out=result[:],
+                in0=lse_total[:, 1:2],
+                scalar1=lse_total[:, 0:1],
+                scalar2=-D * HALF_LOG_2PI,
+                op0=ALU.subtract,
+                op1=ALU.add,
+            )
+            repeated = late.tile([P, P], F32)
+            nc.vector.tensor_copy(out=repeated[:], in_=result[:].to_broadcast([P, P]))
+            as_row = psum_tp.tile([P, P], F32, tag="tp")
+            nc.tensor.transpose(as_row[:], repeated[:], ident[:])
+            row = late.tile([P, P], F32)
+            nc.vector.tensor_copy(out=row[:], in_=as_row[:])
+            nc.sync.dma_start(out=out.rearrange("(o b) -> o b", o=1), in_=row[0:1, :])

@@ -26,7 +26,6 @@ GROUP = 4
 N_GROUPS = D // GROUP
 Y_BANK = 8
 EVERY_VECTOR = 17
-LAG = 2
 HALF_LOG_2PI = 0.5 * math.log(2.0 * math.pi)
 
 FLOPS = 2 * ROWS * ROWS * H * D * 3
@@ -248,10 +247,12 @@ def tile_rnadeoutputlayer_kernel(
                     )
 
             def passes(g):
-                ds = slice(g * GROUP, (g + 1) * GROUP)
                 acc_of[g] = products(g)
                 extra_pass()
-                inv_sigma = work.tile([P, GROUP, ROWS], F32, tag="inv_sigma")
+
+            def make_inv_sigma(g):
+                ds = slice(g * GROUP, (g + 1) * GROUP)
+                inv_sigma = work.tile([P, GROUP, ROWS], F32, tag="inv_sigma", bufs=3)
                 nc.scalar.activation(
                     out=inv_sigma[:], in_=log_sigma[:, ds, :], func=ACT.Exp, scale=-1.0
                 )
@@ -259,7 +260,7 @@ def tile_rnadeoutputlayer_kernel(
 
             def difference(g):
                 acc = acc_of[g]
-                half_z2 = work.tile([P, GROUP, ROWS], F32, tag="half_z2", bufs=LAG + 1)
+                half_z2 = work.tile([P, GROUP, ROWS], F32, tag="half_z2", bufs=3)
                 for i in range(GROUP):
                     d = g * GROUP + i
                     nc.vector.scalar_tensor_tensor(
@@ -272,11 +273,14 @@ def tile_rnadeoutputlayer_kernel(
                     )
                 half_z2_of[g] = half_z2
 
-            def scaled_square(g):
+            def scale(g):
                 half_z2 = half_z2_of[g]
-                nc.vector.tensor_tensor(
+                nc.gpsimd.tensor_tensor(
                     out=half_z2[:], in0=half_z2[:], in1=inv_sigma_of[g][:], op=ALU.mult
                 )
+
+            def square(g):
+                half_z2 = half_z2_of[g]
                 nc.scalar.activation(
                     out=half_z2[:], in_=half_z2[:], func=ACT.Square, scale=math.sqrt(0.5)
                 )
@@ -318,24 +322,32 @@ def tile_rnadeoutputlayer_kernel(
             load_and_quantise(
                 nc, raw_pool, [grouped], D_VECTOR_LATER, V_mu, w_codes, w_scales, alpha_second_half, True
             )
-            with tc.manual_schedule(engines={mybir.EngineType.PE, mybir.EngineType.DVE}):
+            with tc.manual_schedule(
+                engines={mybir.EngineType.PE, mybir.EngineType.DVE, mybir.EngineType.Pool}
+            ):
                 quantise_rest(0)
-                for s in range(N_GROUPS + LAG + 2):
-                    if s + 1 < N_GROUPS:
-                        quantise_rest(s + 1)
+                quantise_rest(1)
+                passes(0)
+                make_inv_sigma(0)
+                for s in range(N_GROUPS + 2):
                     if s < N_GROUPS:
-                        passes(s)
+                        difference(s)
                     if 1 <= s <= N_GROUPS:
-                        scaled_square(s - 1)
-                    if LAG <= s < N_GROUPS + LAG:
-                        exponent(s - LAG)
+                        square(s - 1)
+                    if s + 1 < N_GROUPS:
+                        passes(s + 1)
+                        make_inv_sigma(s + 1)
+                    if s + 2 < N_GROUPS:
+                        quantise_rest(s + 2)
                     if s == N_GROUPS:
                         extra_pass()
                         extra_pass()
-                    if s >= LAG + 1 and s - LAG - 1 < N_GROUPS:
-                        max_and_sum(s - LAG - 1, 1, by_b_of[s - LAG - 1])
+                    if 1 <= s <= N_GROUPS:
+                        exponent(s - 1)
+                    if s >= 2:
+                        max_and_sum(s - 2, 1, by_b_of[s - 2])
                     if s < N_GROUPS:
-                        difference(s)
+                        scale(s)
 
             log_sum = late.tile([P, 2, D], F32)
             log_total = late.tile([P, 2], F32)

@@ -76,7 +76,7 @@ def tile_rnadeoutputlayer_kernel(
     nc = tc.nc
     with (
         tc.tile_pool(name="keep", bufs=1) as keep,
-        tc.tile_pool(name="raw", bufs=7) as raw_pool,
+        tc.tile_pool(name="raw", bufs=8) as raw_pool,
         tc.tile_pool(name="work", bufs=2) as work,
         tc.psum_pool(name="acc", bufs=4) as psum_acc,
         tc.psum_pool(name="tp", bufs=3) as psum_tp,
@@ -145,7 +145,7 @@ def tile_rnadeoutputlayer_kernel(
         def max_and_sum(g, w, by_b):
             ds = slice(g * GROUP, (g + 1) * GROUP)
             nc.vector.tensor_reduce(out=neg_max[:, w, ds], in_=by_b[:], axis=AX.X, op=ALU.min)
-            unused = work.tile([P, GROUP, ROWS], BF16, tag="unused")
+            unused = work.tile([P, GROUP, ROWS], BF16, tag="unused", bufs=1)
             for i in range(GROUP):
                 d = g * GROUP + i
                 nc.scalar.activation(
@@ -252,9 +252,13 @@ def tile_rnadeoutputlayer_kernel(
 
             def make_inv_sigma(g):
                 ds = slice(g * GROUP, (g + 1) * GROUP)
-                inv_sigma = work.tile([P, GROUP, ROWS], F32, tag="inv_sigma", bufs=3)
+                inv_sigma = work.tile([P, GROUP, ROWS], F32, tag="inv_sigma", bufs=2)
                 nc.scalar.activation(
-                    out=inv_sigma[:], in_=log_sigma[:, ds, :], func=ACT.Exp, scale=-1.0
+                    out=inv_sigma[:],
+                    in_=log_sigma[:, ds, :],
+                    func=ACT.Exp,
+                    bias=-0.5 * math.log(2.0),
+                    scale=-1.0,
                 )
                 inv_sigma_of[g] = inv_sigma
 
@@ -275,15 +279,19 @@ def tile_rnadeoutputlayer_kernel(
 
             def scale(g):
                 half_z2 = half_z2_of[g]
-                nc.gpsimd.tensor_tensor(
+                engine = nc.vector if g == N_GROUPS - 1 else nc.gpsimd
+                engine.tensor_tensor(
                     out=half_z2[:], in0=half_z2[:], in1=inv_sigma_of[g][:], op=ALU.mult
                 )
+                if g % 4 == 1:
+                    nc.gpsimd.tensor_tensor(
+                        out=half_z2[:], in0=half_z2[:], in1=half_z2[:], op=ALU.mult
+                    )
 
             def square(g):
                 half_z2 = half_z2_of[g]
-                nc.scalar.activation(
-                    out=half_z2[:], in_=half_z2[:], func=ACT.Square, scale=math.sqrt(0.5)
-                )
+                if g % 4 != 1:
+                    nc.scalar.activation(out=half_z2[:], in_=half_z2[:], func=ACT.Square)
 
             def exponent(g):
                 by_b_of[g] = turn(
@@ -339,6 +347,8 @@ def tile_rnadeoutputlayer_kernel(
                         make_inv_sigma(s + 1)
                     if s + 2 < N_GROUPS:
                         quantise_rest(s + 2)
+                    if N_GROUPS - 2 <= s <= N_GROUPS - 1:
+                        extra_pass()
                     if s == N_GROUPS:
                         extra_pass()
                         extra_pass()
@@ -349,21 +359,12 @@ def tile_rnadeoutputlayer_kernel(
                     if s < N_GROUPS:
                         scale(s)
 
-            log_sum = late.tile([P, 2, D], F32)
-            log_total = late.tile([P, 2], F32)
-            for w in range(2):
-                nc.scalar.activation(
-                    out=log_sum[:, w, :],
-                    in_=exp_sum[:, w, :],
-                    func=ACT.Ln,
-                    accum_out=log_total[:, w : w + 1],
-                )
-            neg_max_total = late.tile([P, 2], F32)
-            nc.vector.tensor_reduce(out=neg_max_total[:], in_=neg_max[:], axis=AX.X, op=ALU.add)
+            log_sum = work.tile([P, 2, D], F32, tag="inv_sigma", bufs=2)
+            nc.scalar.activation(out=log_sum[:], in_=exp_sum[:], func=ACT.Ln)
+            lse = work.tile([P, 2, D], F32, tag="inv_sigma", bufs=2)
+            nc.vector.tensor_tensor(out=lse[:], in0=log_sum[:], in1=neg_max[:], op=ALU.subtract)
             lse_total = late.tile([P, 2], F32)
-            nc.vector.tensor_tensor(
-                out=lse_total[:], in0=log_total[:], in1=neg_max_total[:], op=ALU.subtract
-            )
+            nc.vector.tensor_reduce(out=lse_total[:], in_=lse[:], axis=AX.X, op=ALU.add)
             result = late.tile([P, 1], F32)
             nc.vector.tensor_scalar(
                 out=result[:],
@@ -373,10 +374,10 @@ def tile_rnadeoutputlayer_kernel(
                 op0=ALU.subtract,
                 op1=ALU.add,
             )
-            repeated = late.tile([P, P], F32)
+            repeated = work.tile([P, P], F32, tag="inv_sigma", bufs=2)
             nc.vector.tensor_copy(out=repeated[:], in_=result[:].to_broadcast([P, P]))
             as_row = psum_tp.tile([P, P], F32, tag="tp")
             nc.tensor.transpose(as_row[:], repeated[:], ident[:])
-            row = late.tile([P, P], F32)
+            row = work.tile([P, P], F32, tag="inv_sigma", bufs=2)
             nc.vector.tensor_copy(out=row[:], in_=as_row[:])
             nc.sync.dma_start(out=out.rearrange("(o b) -> o b", o=1), in_=row[0:1, :])

@@ -19,64 +19,30 @@ D = 64
 PACK = 4
 HALF = 64
 CHUNK = 8
+CHUNKS = HALF // CHUNK
+SHARE = D // CHUNKS
 RUN = 4
 D_VECTOR_FIRST = 32
-D_VECTOR_LATER = 40
+D_VECTOR_LATER = 48
+LAG = 2
+LEAD = 4
+AHEAD = 2
 GROUP = 4
 N_GROUPS = D // GROUP
 Y_BANK = 8
-EVERY_VECTOR = 17
 HALF_LOG_2PI = 0.5 * math.log(2.0 * math.pi)
 
 FLOPS = 2 * ROWS * ROWS * H * D * 3
-
-
-def load_and_quantise(
-    nc, raw_pool, grouped_tiles, d_vector, src, codes, scales, other_work=None, leave_last_half=False,
-    small_start=False,
-):
-    by_partition = src.rearrange("r (p j) d -> p r (j d)", j=PACK)
-    for half in range(ROWS // HALF):
-        grouped = grouped_tiles[half % len(grouped_tiles)]
-        sizes = [CHUNK] * (HALF // CHUNK)
-        if small_start and half == 0:
-            sizes = [CHUNK // 4, CHUNK // 4, CHUNK // 2] + sizes[1:]
-        row_in_half = 0
-        for size in sizes:
-            first_row = half * HALF + row_in_half
-            raw = raw_pool.tile([P, size, PACK * D], BF16, tag="raw")
-            nc.sync.dma_start(out=raw[:], in_=by_partition[:, first_row : first_row + size, :])
-            raw_mj = raw[:].rearrange("p r (j d) -> p (r j) d", j=PACK)
-            cols = slice(row_in_half * PACK, (row_in_half + size) * PACK)
-            row_in_half += size
-            for copy, d_range in (
-                (nc.vector.tensor_copy, slice(0, d_vector)),
-                (nc.scalar.copy, slice(d_vector, D)),
-            ):
-                copy(
-                    out=grouped[:, d_range, cols].rearrange("p (c i) m -> p c m i", i=RUN),
-                    in_=raw_mj[:, :, d_range].rearrange("p m (c i) -> p c m i", i=RUN),
-                )
-            if other_work is not None:
-                other_work(first_row // CHUNK)
-        if leave_last_half and half == ROWS // HALF - 1:
-            break
-        rows = slice(half * HALF, (half + 1) * HALF)
-        for d in range(D):
-            nc.vector.quantize_mx(
-                out=codes[:, d, rows].bitcast(FP8X4),
-                scales=scales[:, d, rows],
-                in_=grouped[:, d, :],
-            )
 
 
 def tile_rnadeoutputlayer_kernel(
     tc, x, input_var, V_alpha, V_mu, V_sigma, b_alpha, b_mu, b_sigma, out
 ):
     nc = tc.nc
+    engines = mybir.EngineType
     with (
         tc.tile_pool(name="keep", bufs=1) as keep,
-        tc.tile_pool(name="raw", bufs=8) as raw_pool,
+        tc.tile_pool(name="raw", bufs=7) as raw_pool,
         tc.tile_pool(name="work", bufs=2) as work,
         tc.psum_pool(name="acc", bufs=4) as psum_acc,
         tc.psum_pool(name="tp", bufs=3) as psum_tp,
@@ -96,11 +62,6 @@ def tile_rnadeoutputlayer_kernel(
         bias_sigma = keep.tile([P, D], F32)
         bias_mu = keep.tile([P, D], F32)
         neg_bias_alpha = keep.tile([P, D], F32)
-        nc.vector.tensor_copy(out=bias_sigma[:], in_=bias_bf[:, 0, :])
-        nc.vector.tensor_copy(out=bias_mu[:], in_=bias_bf[:, 1, :])
-        nc.vector.tensor_scalar(
-            out=neg_bias_alpha[:], in0=bias_bf[:, 2, :], scalar1=-1.0, scalar2=None, op0=ALU.mult
-        )
 
         grouped = keep.tile([P, D, HALF * PACK], BF16, align_bytes=64)
         x_codes = keep.tile([P, D, ROWS], U32, align_bytes=64)
@@ -111,6 +72,34 @@ def tile_rnadeoutputlayer_kernel(
         y_all = keep.tile([P, D, ROWS], BF16)
         neg_max = keep.tile([P, 2, D], F32)
         exp_sum = keep.tile([P, 2, D], F32)
+
+        def regroup(src, first_row, rows, tile, d_vector):
+            by_partition = src.rearrange("r (p j) d -> p r (j d)", j=PACK)
+            raw = raw_pool.tile([P, rows, PACK * D], BF16, tag="raw")
+            nc.sync.dma_start(out=raw[:], in_=by_partition[:, first_row : first_row + rows, :])
+            raw_mj = raw[:].rearrange("p r (j d) -> p (r j) d", j=PACK)
+            first = first_row % HALF
+            cols = slice(first * PACK, (first + rows) * PACK)
+            for copy, d_range in (
+                (nc.vector.tensor_copy, slice(0, d_vector)),
+                (nc.scalar.copy, slice(d_vector, D)),
+            ):
+                copy(
+                    out=tile[:, d_range, cols].rearrange("p (c i) m -> p c m i", i=RUN),
+                    in_=raw_mj[:, :, d_range].rearrange("p m (c i) -> p c m i", i=RUN),
+                )
+
+        def quantise(ds, half, tile, codes, scales):
+            rows = slice(half * HALF, (half + 1) * HALF)
+            for d in ds:
+                nc.vector.quantize_mx(
+                    out=codes[:, d, rows].bitcast(FP8X4),
+                    scales=scales[:, d, rows],
+                    in_=tile[:, d, :],
+                )
+
+        def share(c):
+            return range(c * SHARE, (c + 1) * SHARE)
 
         def products(g):
             acc = psum_acc.tile([P, GROUP, ROWS], F32, tag="acc")
@@ -127,6 +116,17 @@ def tile_rnadeoutputlayer_kernel(
                 )
             return acc
 
+        def add_bias(g, acc, target, bias, scale):
+            for i in range(GROUP):
+                d = g * GROUP + i
+                nc.scalar.activation(
+                    out=target[:, d, :],
+                    in_=acc[:, i, :],
+                    func=ACT.Identity,
+                    bias=bias[:, d : d + 1],
+                    scale=scale,
+                )
+
         def turn(terms_of):
             by_b = psum_tp.tile([P, GROUP, ROWS], F32, tag="tp")
             for i in range(GROUP):
@@ -142,10 +142,12 @@ def tile_rnadeoutputlayer_kernel(
                     )
             return by_b
 
-        def max_and_sum(g, w, by_b):
+        def minimum(g, w, by_b):
             ds = slice(g * GROUP, (g + 1) * GROUP)
             nc.vector.tensor_reduce(out=neg_max[:, w, ds], in_=by_b[:], axis=AX.X, op=ALU.min)
-            unused = work.tile([P, GROUP, ROWS], BF16, tag="unused", bufs=1)
+
+        def exp_and_sum(g, w, by_b):
+            unused = work.tile([P, GROUP, ROWS], BF16, tag="unused")
             for i in range(GROUP):
                 d = g * GROUP + i
                 nc.scalar.activation(
@@ -157,75 +159,84 @@ def tile_rnadeoutputlayer_kernel(
                     accum_out=exp_sum[:, w, d : d + 1],
                 )
 
-        def reduce_over_k(g, w, terms_of):
-            max_and_sum(g, w, turn(terms_of))
-
-        for first in range(0, D, Y_BANK):
-            spread = psum_acc.tile([P, Y_BANK, ROWS], BF16, tag="acc")
+        def spread_y(first):
+            bank = psum_acc.tile([P, Y_BANK, ROWS], BF16, tag="acc")
             for i in range(Y_BANK):
                 d = first + i
                 nc.tensor.matmul(
-                    out=spread[:, i, :],
+                    out=bank[:, i, :],
                     lhsT=y_bf[:, d : d + 1].to_broadcast([P, P]),
                     rhs=ident_bf[:],
                     start=True,
                     stop=True,
                 )
-            nc.vector.tensor_copy(out=y_all[:, first : first + Y_BANK, :], in_=spread[:])
+            nc.vector.tensor_copy(out=y_all[:, first : first + Y_BANK, :], in_=bank[:])
 
-        with tc.tile_pool(name="early", bufs=1) as early:
+        ordered = {engines.PE, engines.DVE, engines.Activation, engines.Pool}
+        with tc.tile_pool(name="early", bufs=1) as early, tc.manual_schedule(engines=ordered):
             grouped_too = early.tile([P, D, HALF * PACK], BF16, align_bytes=64)
-            two_grouped = [grouped, grouped_too]
+            acc_of = {}
 
-            load_and_quantise(
-                nc, raw_pool, two_grouped, D_VECTOR_FIRST, x, x_codes, x_scales, None, False, True
-            )
-            load_and_quantise(
-                nc, raw_pool, two_grouped, D_VECTOR_FIRST, V_alpha, w_codes, w_scales
+            for first_row, rows in ((0, 2), (2, 2), (4, 4)):
+                regroup(x, first_row, rows, grouped, D_VECTOR_FIRST)
+            for c in range(1, CHUNKS):
+                regroup(x, c * CHUNK, CHUNK, grouped, D_VECTOR_FIRST)
+                spread_y((c - 1) * Y_BANK)
+            for c in range(CHUNKS):
+                regroup(x, HALF + c * CHUNK, CHUNK, grouped_too, D_VECTOR_FIRST)
+                quantise(share(c), 0, grouped, x_codes, x_scales)
+            spread_y((CHUNKS - 1) * Y_BANK)
+            nc.vector.tensor_copy(out=bias_sigma[:], in_=bias_bf[:, 0, :])
+            nc.vector.tensor_copy(out=bias_mu[:], in_=bias_bf[:, 1, :])
+            nc.vector.tensor_scalar(
+                out=neg_bias_alpha[:],
+                in0=bias_bf[:, 2, :],
+                scalar1=-1.0,
+                scalar2=None,
+                op0=ALU.mult,
             )
 
+            for c in range(CHUNKS):
+                regroup(V_alpha, c * CHUNK, CHUNK, grouped, D_VECTOR_FIRST)
+                quantise(share(c), 1, grouped_too, x_codes, x_scales)
+            for c in range(CHUNKS):
+                regroup(V_alpha, HALF + c * CHUNK, CHUNK, grouped_too, D_VECTOR_FIRST)
+                quantise(share(c), 0, grouped, w_codes, w_scales)
+
+            for c in range(CHUNKS):
+                regroup(V_sigma, c * CHUNK, CHUNK, grouped, D_VECTOR_LATER)
+                quantise(share(c), 1, grouped_too, w_codes, w_scales)
+                for g in (2 * c, 2 * c + 1):
+                    add_bias(g, products(g), neg_a, neg_bias_alpha, -1.0)
+            by_b_of = {}
+            for c in range(CHUNKS):
+                by_b_of[c] = turn(lambda i: [neg_a[:, c * GROUP + i, :]])
+                regroup(V_sigma, HALF + c * CHUNK, CHUNK, grouped_too, D_VECTOR_LATER)
+                quantise(share(c), 0, grouped, w_codes, w_scales)
+                if c >= LAG:
+                    minimum(c - LAG, 0, by_b_of[c - LAG])
+                    exp_and_sum(c - LAG, 0, by_b_of[c - LAG])
+            for g in range(CHUNKS - LAG, CHUNKS):
+                minimum(g, 0, by_b_of[g])
             for g in range(N_GROUPS):
-                acc = products(g)
-                for i in range(GROUP):
-                    d = g * GROUP + i
-                    if g % EVERY_VECTOR != EVERY_VECTOR - 1:
-                        nc.scalar.activation(
-                            out=neg_a[:, d, :],
-                            in_=acc[:, i, :],
-                            func=ACT.Identity,
-                            bias=neg_bias_alpha[:, d : d + 1],
-                            scale=-1.0,
-                        )
-                    else:
-                        nc.vector.tensor_scalar(
-                            out=neg_a[:, d, :],
-                            in0=acc[:, i, :],
-                            scalar1=-1.0,
-                            scalar2=neg_bias_alpha[:, d : d + 1],
-                            op0=ALU.mult,
-                            op1=ALU.add,
-                        )
+                quantise(range(g * GROUP, (g + 1) * GROUP), 1, grouped_too, w_codes, w_scales)
 
-            def alpha_group(g):
-                reduce_over_k(g, 0, lambda i: [neg_a[:, g * GROUP + i, :]])
-
-            def alpha_first_half(step):
-                if step % 2 == 0:
-                    alpha_group(step // 2)
-
-            load_and_quantise(
-                nc, raw_pool, two_grouped, D_VECTOR_LATER, V_sigma, w_codes, w_scales, alpha_first_half
-            )
-
-        with tc.tile_pool(name="late", bufs=1) as late:
+        with tc.tile_pool(name="late", bufs=1) as late, tc.manual_schedule(engines=ordered):
             log_sigma = late.tile([P, D, ROWS], F32)
-
             spare = psum_spare.tile([P, GROUP * ROWS], F32)
             half_z2_of = {}
             inv_sigma_of = {}
 
-            acc_of = {}
-            by_b_of = {}
+            def clip(g):
+                ds = slice(g * GROUP, (g + 1) * GROUP)
+                nc.vector.tensor_scalar(
+                    out=log_sigma[:, ds, :],
+                    in0=log_sigma[:, ds, :],
+                    scalar1=-20.0,
+                    scalar2=20.0,
+                    op0=ALU.max,
+                    op1=ALU.min,
+                )
 
             def extra_pass():
                 nc.tensor.matmul_mx(
@@ -238,21 +249,13 @@ def tile_rnadeoutputlayer_kernel(
                     stop=True,
                 )
 
-            def quantise_rest(g):
-                for d in range(g * GROUP, (g + 1) * GROUP):
-                    nc.vector.quantize_mx(
-                        out=w_codes[:, d, HALF:ROWS].bitcast(FP8X4),
-                        scales=w_scales[:, d, HALF:ROWS],
-                        in_=grouped[:, d, :],
-                    )
-
             def passes(g):
                 acc_of[g] = products(g)
                 extra_pass()
 
-            def make_inv_sigma(g):
+            def invert(g):
                 ds = slice(g * GROUP, (g + 1) * GROUP)
-                inv_sigma = work.tile([P, GROUP, ROWS], F32, tag="inv_sigma", bufs=2)
+                inv_sigma = work.tile([P, GROUP, ROWS], F32, tag="inv_sigma", bufs=AHEAD + 1)
                 nc.scalar.activation(
                     out=inv_sigma[:],
                     in_=log_sigma[:, ds, :],
@@ -302,82 +305,94 @@ def tile_rnadeoutputlayer_kernel(
                     ]
                 )
 
-            for g in range(N_GROUPS):
-                ds = slice(g * GROUP, (g + 1) * GROUP)
-                acc = products(g)
-                for i in range(GROUP):
-                    d = g * GROUP + i
-                    nc.scalar.activation(
-                        out=log_sigma[:, d, :],
-                        in_=acc[:, i, :],
-                        func=ACT.Identity,
-                        bias=bias_sigma[:, d : d + 1],
-                        scale=1.0,
-                    )
-                nc.vector.tensor_scalar(
-                    out=log_sigma[:, ds, :],
-                    in0=log_sigma[:, ds, :],
-                    scalar1=-20.0,
-                    scalar2=20.0,
-                    op0=ALU.max,
-                    op1=ALU.min,
-                )
+            def sigma_pair(n):
+                for g in (2 * n, 2 * n + 1):
+                    add_bias(g, products(g), log_sigma, bias_sigma, 1.0)
+                    if g >= 2:
+                        clip(g - 2)
 
-            def alpha_second_half(step):
-                if step % 2 == 0:
-                    alpha_group(N_GROUPS // 2 + step // 2)
+            for c in range(CHUNKS):
+                regroup(V_mu, c * CHUNK, CHUNK, grouped, D_VECTOR_LATER)
+                if c < LAG:
+                    exp_and_sum(CHUNKS - LAG + c, 0, by_b_of[CHUNKS - LAG + c])
+                if c >= LEAD:
+                    sigma_pair(c - LEAD)
+            for n in range(CHUNKS - LEAD, CHUNKS):
+                sigma_pair(n)
+            quantise(range(D_VECTOR_LATER, D), 0, grouped, w_codes, w_scales)
+            quantise(range(0, D_VECTOR_LATER), 0, grouped, w_codes, w_scales)
+            clip(N_GROUPS - 2)
+            clip(N_GROUPS - 1)
+            for g in range(AHEAD):
+                invert(g)
+            for c in range(CHUNKS):
+                g = CHUNKS + c
+                by_b_of[g] = turn(lambda i: [neg_a[:, g * GROUP + i, :]])
+                regroup(V_mu, HALF + c * CHUNK, CHUNK, grouped, D_VECTOR_LATER)
+                minimum(g, 0, by_b_of[g])
+                exp_and_sum(g, 0, by_b_of[g])
 
-            load_and_quantise(
-                nc, raw_pool, [grouped], D_VECTOR_LATER, V_mu, w_codes, w_scales, alpha_second_half, True
+            def quantise_rest(g):
+                quantise(range(g * GROUP, (g + 1) * GROUP), 1, grouped, w_codes, w_scales)
+
+            quantise_rest(0)
+            quantise_rest(1)
+            passes(0)
+            for s in range(N_GROUPS + 2):
+                if s < N_GROUPS:
+                    difference(s)
+                    scale(s)
+                if 1 <= s <= N_GROUPS:
+                    square(s - 1)
+                if s + 1 < N_GROUPS:
+                    passes(s + 1)
+                if s + AHEAD < N_GROUPS:
+                    invert(s + AHEAD)
+                if s + 2 < N_GROUPS:
+                    quantise_rest(s + 2)
+                if s == N_GROUPS:
+                    extra_pass()
+                    extra_pass()
+                if 1 <= s <= N_GROUPS:
+                    exponent(s - 1)
+                if s >= 2:
+                    minimum(s - 2, 1, by_b_of[s - 2])
+                    exp_and_sum(s - 2, 1, by_b_of[s - 2])
+
+            max_part = late.tile([P, D], F32)
+            nc.vector.tensor_tensor(
+                out=max_part[:], in0=neg_max[:, 0, :], in1=neg_max[:, 1, :], op=ALU.subtract
             )
-            with tc.manual_schedule(
-                engines={mybir.EngineType.PE, mybir.EngineType.DVE, mybir.EngineType.Pool}
-            ):
-                quantise_rest(0)
-                quantise_rest(1)
-                passes(0)
-                make_inv_sigma(0)
-                for s in range(N_GROUPS + 2):
-                    if s < N_GROUPS:
-                        difference(s)
-                    if 1 <= s <= N_GROUPS:
-                        square(s - 1)
-                    if s + 1 < N_GROUPS:
-                        passes(s + 1)
-                        make_inv_sigma(s + 1)
-                    if s + 2 < N_GROUPS:
-                        quantise_rest(s + 2)
-                    if N_GROUPS - 2 <= s <= N_GROUPS - 1:
-                        extra_pass()
-                    if s == N_GROUPS:
-                        extra_pass()
-                        extra_pass()
-                    if 1 <= s <= N_GROUPS:
-                        exponent(s - 1)
-                    if s >= 2:
-                        max_and_sum(s - 2, 1, by_b_of[s - 2])
-                    if s < N_GROUPS:
-                        scale(s)
-
-            log_sum = work.tile([P, 2, D], F32, tag="inv_sigma", bufs=2)
-            nc.scalar.activation(out=log_sum[:], in_=exp_sum[:], func=ACT.Ln)
-            lse = work.tile([P, 2, D], F32, tag="inv_sigma", bufs=2)
-            nc.vector.tensor_tensor(out=lse[:], in0=log_sum[:], in1=neg_max[:], op=ALU.subtract)
-            lse_total = late.tile([P, 2], F32)
-            nc.vector.tensor_reduce(out=lse_total[:], in_=lse[:], axis=AX.X, op=ALU.add)
-            result = late.tile([P, 1], F32)
+            max_total = late.tile([P, 1], F32)
+            nc.vector.tensor_reduce(out=max_total[:], in_=max_part[:], axis=AX.X, op=ALU.add)
+            constant = late.tile([P, 1], F32)
             nc.vector.tensor_scalar(
-                out=result[:],
-                in0=lse_total[:, 1:2],
-                scalar1=lse_total[:, 0:1],
-                scalar2=-D * HALF_LOG_2PI,
+                out=constant[:],
+                in0=max_total[:],
+                scalar1=-D * HALF_LOG_2PI,
+                scalar2=None,
+                op0=ALU.add,
+            )
+            log_sum = late.tile([P, 2, D], F32)
+            log_total = late.tile([P, 2], F32)
+            for w in range(2):
+                nc.scalar.activation(
+                    out=log_sum[:, w, :],
+                    in_=exp_sum[:, w, :],
+                    func=ACT.Ln,
+                    accum_out=log_total[:, w : w + 1],
+                )
+            repeated = work.tile([P, P], F32, tag="half_z2", bufs=3)
+            nc.vector.tensor_scalar(
+                out=repeated[:],
+                in0=log_total[:, 1:2].to_broadcast([P, P]),
+                scalar1=log_total[:, 0:1],
+                scalar2=constant[:],
                 op0=ALU.subtract,
                 op1=ALU.add,
             )
-            repeated = work.tile([P, P], F32, tag="inv_sigma", bufs=2)
-            nc.vector.tensor_copy(out=repeated[:], in_=result[:].to_broadcast([P, P]))
             as_row = psum_tp.tile([P, P], F32, tag="tp")
             nc.tensor.transpose(as_row[:], repeated[:], ident[:])
-            row = work.tile([P, P], F32, tag="inv_sigma", bufs=2)
+            row = work.tile([P, P], F32, tag="half_z2", bufs=3)
             nc.vector.tensor_copy(out=row[:], in_=as_row[:])
             nc.sync.dma_start(out=out.rearrange("(o b) -> o b", o=1), in_=row[0:1, :])

@@ -22,8 +22,9 @@ CHUNK = 8
 CHUNKS = HALF // CHUNK
 SHARE = D // CHUNKS
 RUN = 4
-D_VECTOR_FIRST = 32
-D_VECTOR_LATER = 48
+D_VECTOR_FIRST = (32, 24)
+D_VECTOR_SIGMA = (40, 48)
+D_VECTOR_MU = 40
 LAG = 2
 LEAD = 4
 AHEAD = 2
@@ -178,12 +179,12 @@ def tile_rnadeoutputlayer_kernel(
             acc_of = {}
 
             for first_row, rows in ((0, 2), (2, 2), (4, 4)):
-                regroup(x, first_row, rows, grouped, D_VECTOR_FIRST)
+                regroup(x, first_row, rows, grouped, D_VECTOR_FIRST[0])
             for c in range(1, CHUNKS):
-                regroup(x, c * CHUNK, CHUNK, grouped, D_VECTOR_FIRST)
+                regroup(x, c * CHUNK, CHUNK, grouped, D_VECTOR_FIRST[c % 2])
                 spread_y((c - 1) * Y_BANK)
             for c in range(CHUNKS):
-                regroup(x, HALF + c * CHUNK, CHUNK, grouped_too, D_VECTOR_FIRST)
+                regroup(x, HALF + c * CHUNK, CHUNK, grouped_too, D_VECTOR_FIRST[c % 2])
                 quantise(share(c), 0, grouped, x_codes, x_scales)
             spread_y((CHUNKS - 1) * Y_BANK)
             nc.vector.tensor_copy(out=bias_sigma[:], in_=bias_bf[:, 0, :])
@@ -197,21 +198,21 @@ def tile_rnadeoutputlayer_kernel(
             )
 
             for c in range(CHUNKS):
-                regroup(V_alpha, c * CHUNK, CHUNK, grouped, D_VECTOR_FIRST)
+                regroup(V_alpha, c * CHUNK, CHUNK, grouped, D_VECTOR_FIRST[c % 2])
                 quantise(share(c), 1, grouped_too, x_codes, x_scales)
             for c in range(CHUNKS):
-                regroup(V_alpha, HALF + c * CHUNK, CHUNK, grouped_too, D_VECTOR_FIRST)
+                regroup(V_alpha, HALF + c * CHUNK, CHUNK, grouped_too, D_VECTOR_FIRST[c % 2])
                 quantise(share(c), 0, grouped, w_codes, w_scales)
 
             for c in range(CHUNKS):
-                regroup(V_sigma, c * CHUNK, CHUNK, grouped, D_VECTOR_LATER)
+                regroup(V_sigma, c * CHUNK, CHUNK, grouped, D_VECTOR_SIGMA[c % 2])
                 quantise(share(c), 1, grouped_too, w_codes, w_scales)
                 for g in (2 * c, 2 * c + 1):
                     add_bias(g, products(g), neg_a, neg_bias_alpha, -1.0)
             by_b_of = {}
             for c in range(CHUNKS):
                 by_b_of[c] = turn(lambda i: [neg_a[:, c * GROUP + i, :]])
-                regroup(V_sigma, HALF + c * CHUNK, CHUNK, grouped_too, D_VECTOR_LATER)
+                regroup(V_sigma, HALF + c * CHUNK, CHUNK, grouped_too, D_VECTOR_SIGMA[c % 2])
                 quantise(share(c), 0, grouped, w_codes, w_scales)
                 if c >= LAG:
                     minimum(c - LAG, 0, by_b_of[c - LAG])
@@ -282,18 +283,18 @@ def tile_rnadeoutputlayer_kernel(
 
             def scale(g):
                 half_z2 = half_z2_of[g]
-                engine = nc.vector if g == N_GROUPS - 1 else nc.gpsimd
+                engine = nc.vector if g % 4 == 3 else nc.gpsimd
                 engine.tensor_tensor(
                     out=half_z2[:], in0=half_z2[:], in1=inv_sigma_of[g][:], op=ALU.mult
                 )
-                if g % 4 == 1:
+                if g % 4 == 3 and g < N_GROUPS - 1:
                     nc.gpsimd.tensor_tensor(
                         out=half_z2[:], in0=half_z2[:], in1=half_z2[:], op=ALU.mult
                     )
 
             def square(g):
                 half_z2 = half_z2_of[g]
-                if g % 4 != 1:
+                if g % 4 != 3 or g == N_GROUPS - 1:
                     nc.scalar.activation(out=half_z2[:], in_=half_z2[:], func=ACT.Square)
 
             def exponent(g):
@@ -312,15 +313,15 @@ def tile_rnadeoutputlayer_kernel(
                         clip(g - 2)
 
             for c in range(CHUNKS):
-                regroup(V_mu, c * CHUNK, CHUNK, grouped, D_VECTOR_LATER)
+                regroup(V_mu, c * CHUNK, CHUNK, grouped, D_VECTOR_MU)
                 if c < LAG:
                     exp_and_sum(CHUNKS - LAG + c, 0, by_b_of[CHUNKS - LAG + c])
                 if c >= LEAD:
                     sigma_pair(c - LEAD)
             for n in range(CHUNKS - LEAD, CHUNKS):
                 sigma_pair(n)
-            quantise(range(D_VECTOR_LATER, D), 0, grouped, w_codes, w_scales)
-            quantise(range(0, D_VECTOR_LATER), 0, grouped, w_codes, w_scales)
+            quantise(range(D_VECTOR_MU, D), 0, grouped, w_codes, w_scales)
+            quantise(range(0, D_VECTOR_MU), 0, grouped, w_codes, w_scales)
             clip(N_GROUPS - 2)
             clip(N_GROUPS - 1)
             for g in range(AHEAD):
@@ -328,7 +329,7 @@ def tile_rnadeoutputlayer_kernel(
             for c in range(CHUNKS):
                 g = CHUNKS + c
                 by_b_of[g] = turn(lambda i: [neg_a[:, g * GROUP + i, :]])
-                regroup(V_mu, HALF + c * CHUNK, CHUNK, grouped, D_VECTOR_LATER)
+                regroup(V_mu, HALF + c * CHUNK, CHUNK, grouped, D_VECTOR_MU)
                 minimum(g, 0, by_b_of[g])
                 exp_and_sum(g, 0, by_b_of[g])
 
@@ -350,6 +351,8 @@ def tile_rnadeoutputlayer_kernel(
                     invert(s + AHEAD)
                 if s + 2 < N_GROUPS:
                     quantise_rest(s + 2)
+                if N_GROUPS - 2 <= s < N_GROUPS:
+                    extra_pass()
                 if s == N_GROUPS:
                     extra_pass()
                     extra_pass()

@@ -25,6 +25,7 @@ RUN = 4
 D_VECTOR_FIRST = (32, 24)
 D_VECTOR_SIGMA = (40, 48)
 D_VECTOR_MU = 40
+D_TENSOR_MU = 16
 LAG = 2
 LEAD = 4
 AHEAD = 2
@@ -74,21 +75,33 @@ def tile_rnadeoutputlayer_kernel(
         neg_max = keep.tile([P, 2, D], F32)
         exp_sum = keep.tile([P, 2, D], F32)
 
-        def regroup(src, first_row, rows, tile, d_vector):
+        def regroup(src, first_row, rows, tile, d_vector, d_tensor=0):
             by_partition = src.rearrange("r (p j) d -> p r (j d)", j=PACK)
             raw = raw_pool.tile([P, rows, PACK * D], BF16, tag="raw")
             nc.sync.dma_start(out=raw[:], in_=by_partition[:, first_row : first_row + rows, :])
             raw_mj = raw[:].rearrange("p r (j d) -> p (r j) d", j=PACK)
             first = first_row % HALF
             cols = slice(first * PACK, (first + rows) * PACK)
+            d_scalar = d_vector + d_tensor
+            if d_tensor > 0:
+                bank = psum_spare.tile([P, d_tensor, rows * PACK], BF16, tag="spare")
+                nc.tensor.matmul(
+                    out=bank[:].rearrange("p d m -> p m d"),
+                    lhsT=ident_bf[:],
+                    rhs=raw_mj[:, :, d_vector:d_scalar],
+                    start=True,
+                    stop=True,
+                )
             for copy, d_range in (
                 (nc.vector.tensor_copy, slice(0, d_vector)),
-                (nc.scalar.copy, slice(d_vector, D)),
+                (nc.scalar.copy, slice(d_scalar, D)),
             ):
                 copy(
                     out=tile[:, d_range, cols].rearrange("p (c i) m -> p c m i", i=RUN),
                     in_=raw_mj[:, :, d_range].rearrange("p m (c i) -> p c m i", i=RUN),
                 )
+            if d_tensor > 0:
+                nc.scalar.copy(out=tile[:, d_vector:d_scalar, cols], in_=bank[:])
 
         def quantise(ds, half, tile, codes, scales):
             rows = slice(half * HALF, (half + 1) * HALF)
@@ -168,6 +181,7 @@ def tile_rnadeoutputlayer_kernel(
                     out=bank[:, i, :],
                     lhsT=y_bf[:, d : d + 1].to_broadcast([P, P]),
                     rhs=ident_bf[:],
+                    is_transpose=True,
                     start=True,
                     stop=True,
                 )
@@ -224,7 +238,7 @@ def tile_rnadeoutputlayer_kernel(
 
         with tc.tile_pool(name="late", bufs=1) as late, tc.manual_schedule(engines=ordered):
             log_sigma = late.tile([P, D, ROWS], F32)
-            spare = psum_spare.tile([P, GROUP * ROWS], F32)
+            spare = psum_spare.tile([P, GROUP * ROWS], F32, tag="spare")
             half_z2_of = {}
             inv_sigma_of = {}
 
@@ -313,7 +327,7 @@ def tile_rnadeoutputlayer_kernel(
                         clip(g - 2)
 
             for c in range(CHUNKS):
-                regroup(V_mu, c * CHUNK, CHUNK, grouped, D_VECTOR_MU)
+                regroup(V_mu, c * CHUNK, CHUNK, grouped, D_VECTOR_MU, D_TENSOR_MU)
                 if c < LAG:
                     exp_and_sum(CHUNKS - LAG + c, 0, by_b_of[CHUNKS - LAG + c])
                 if c >= LEAD:
@@ -329,7 +343,7 @@ def tile_rnadeoutputlayer_kernel(
             for c in range(CHUNKS):
                 g = CHUNKS + c
                 by_b_of[g] = turn(lambda i: [neg_a[:, g * GROUP + i, :]])
-                regroup(V_mu, HALF + c * CHUNK, CHUNK, grouped, D_VECTOR_MU)
+                regroup(V_mu, HALF + c * CHUNK, CHUNK, grouped, D_VECTOR_MU, D_TENSOR_MU)
                 minimum(g, 0, by_b_of[g])
                 exp_and_sum(g, 0, by_b_of[g])
 

@@ -28,6 +28,7 @@ D_VECTOR_MU = 40
 D_TENSOR_MU = 16
 LAG = 2
 LEAD = 4
+EARLY = 1
 AHEAD = 2
 GROUP = 4
 N_GROUPS = D // GROUP
@@ -46,9 +47,8 @@ def tile_rnadeoutputlayer_kernel(
         tc.tile_pool(name="keep", bufs=1) as keep,
         tc.tile_pool(name="raw", bufs=7) as raw_pool,
         tc.tile_pool(name="work", bufs=2) as work,
-        tc.psum_pool(name="acc", bufs=4) as psum_acc,
-        tc.psum_pool(name="tp", bufs=3) as psum_tp,
-        tc.psum_pool(name="spare", bufs=1) as psum_spare,
+        tc.psum_pool(name="acc", bufs=3) as psum_acc,
+        tc.psum_pool(name="tp", bufs=5) as psum_tp,
     ):
         ident = keep.tile([P, P], F32)
         make_identity(nc, ident[:])
@@ -84,7 +84,7 @@ def tile_rnadeoutputlayer_kernel(
             cols = slice(first * PACK, (first + rows) * PACK)
             d_scalar = d_vector + d_tensor
             if d_tensor > 0:
-                bank = psum_spare.tile([P, d_tensor, rows * PACK], BF16, tag="spare")
+                bank = psum_tp.tile([P, d_tensor, rows * PACK], BF16, tag="tp")
                 nc.tensor.matmul(
                     out=bank[:].rearrange("p d m -> p m d"),
                     lhsT=ident_bf[:],
@@ -115,8 +115,21 @@ def tile_rnadeoutputlayer_kernel(
         def share(c):
             return range(c * SHARE, (c + 1) * SHARE)
 
-        def products(g):
+        def extra_pass(acc):
+            nc.tensor.matmul_mx(
+                out=acc[:].rearrange("p d b -> p (d b)"),
+                lhsT=x_codes[:, 0, :].bitcast(FP8X4),
+                lhsT_scale=x_scales[:, 0, :],
+                rhs=x_codes[:, 0:GROUP, :].rearrange("p d r -> p (d r)").bitcast(FP8X4),
+                rhs_scale=x_scales[:, 0:GROUP, :].rearrange("p d r -> p (d r)"),
+                start=True,
+                stop=True,
+            )
+
+        def products(g, extra=False):
             acc = psum_acc.tile([P, GROUP, ROWS], F32, tag="acc")
+            if extra:
+                extra_pass(acc)
             for i in range(GROUP):
                 d = g * GROUP + i
                 nc.tensor.matmul_mx(
@@ -238,7 +251,6 @@ def tile_rnadeoutputlayer_kernel(
 
         with tc.tile_pool(name="late", bufs=1) as late, tc.manual_schedule(engines=ordered):
             log_sigma = late.tile([P, D, ROWS], F32)
-            spare = psum_spare.tile([P, GROUP * ROWS], F32, tag="spare")
             half_z2_of = {}
             inv_sigma_of = {}
 
@@ -253,20 +265,8 @@ def tile_rnadeoutputlayer_kernel(
                     op1=ALU.min,
                 )
 
-            def extra_pass():
-                nc.tensor.matmul_mx(
-                    out=spare[:],
-                    lhsT=x_codes[:, 0, :].bitcast(FP8X4),
-                    lhsT_scale=x_scales[:, 0, :],
-                    rhs=x_codes[:, 0:GROUP, :].rearrange("p d r -> p (d r)").bitcast(FP8X4),
-                    rhs_scale=x_scales[:, 0:GROUP, :].rearrange("p d r -> p (d r)"),
-                    start=True,
-                    stop=True,
-                )
-
             def passes(g):
-                acc_of[g] = products(g)
-                extra_pass()
+                acc_of[g] = products(g, True)
 
             def invert(g):
                 ds = slice(g * GROUP, (g + 1) * GROUP)
@@ -311,14 +311,26 @@ def tile_rnadeoutputlayer_kernel(
                 if g % 4 != 3 or g == N_GROUPS - 1:
                     nc.scalar.activation(out=half_z2[:], in_=half_z2[:], func=ACT.Square)
 
-            def exponent(g):
-                by_b_of[g] = turn(
-                    lambda i: [
-                        neg_a[:, g * GROUP + i, :],
-                        log_sigma[:, g * GROUP + i, :],
-                        half_z2_of[g][:, i, :],
-                    ]
+            def flip(by_b, i, term, start, stop):
+                nc.tensor.matmul(
+                    out=by_b[:, i, :],
+                    lhsT=term,
+                    rhs=ident[:],
+                    is_transpose=True,
+                    start=start,
+                    stop=stop,
                 )
+
+            def begin_exponent(g):
+                by_b = psum_tp.tile([P, GROUP, ROWS], F32, tag="tp")
+                for i in range(GROUP):
+                    flip(by_b, i, neg_a[:, g * GROUP + i, :], i == 0, False)
+                    flip(by_b, i, log_sigma[:, g * GROUP + i, :], False, False)
+                by_b_of[g] = by_b
+
+            def end_exponent(g):
+                for i in range(GROUP):
+                    flip(by_b_of[g], i, half_z2_of[g][:, i, :], False, i == GROUP - 1)
 
             def sigma_pair(n):
                 for g in (2 * n, 2 * n + 1):
@@ -345,11 +357,16 @@ def tile_rnadeoutputlayer_kernel(
                 by_b_of[g] = turn(lambda i: [neg_a[:, g * GROUP + i, :]])
                 regroup(V_mu, HALF + c * CHUNK, CHUNK, grouped, D_VECTOR_MU, D_TENSOR_MU)
                 minimum(g, 0, by_b_of[g])
+                if c >= LAG:
+                    exp_and_sum(g - LAG, 0, by_b_of[g - LAG])
+            for g in range(N_GROUPS - LAG, N_GROUPS):
                 exp_and_sum(g, 0, by_b_of[g])
 
             def quantise_rest(g):
                 quantise(range(g * GROUP, (g + 1) * GROUP), 1, grouped, w_codes, w_scales)
 
+            for g in range(EARLY):
+                begin_exponent(g)
             quantise_rest(0)
             quantise_rest(1)
             passes(0)
@@ -366,12 +383,14 @@ def tile_rnadeoutputlayer_kernel(
                 if s + 2 < N_GROUPS:
                     quantise_rest(s + 2)
                 if N_GROUPS - 2 <= s < N_GROUPS:
-                    extra_pass()
+                    extra_pass(psum_acc.tile([P, GROUP, ROWS], F32, tag="acc", name="unread"))
                 if s == N_GROUPS:
-                    extra_pass()
-                    extra_pass()
+                    extra_pass(psum_acc.tile([P, GROUP, ROWS], F32, tag="acc", name="unread"))
+                    extra_pass(psum_acc.tile([P, GROUP, ROWS], F32, tag="acc", name="unread"))
                 if 1 <= s <= N_GROUPS:
-                    exponent(s - 1)
+                    end_exponent(s - 1)
+                if s + EARLY < N_GROUPS:
+                    begin_exponent(s + EARLY)
                 if s >= 2:
                     minimum(s - 2, 1, by_b_of[s - 2])
                     exp_and_sum(s - 2, 1, by_b_of[s - 2])

@@ -24,8 +24,9 @@ SHARE = D // CHUNKS
 RUN = 4
 D_VECTOR_FIRST = (32, 24)
 D_VECTOR_SIGMA = (40, 48)
-D_VECTOR_MU = 40
-D_TENSOR_MU = 16
+D_VECTOR_MU = (40, 32)
+D_TENSOR_MU = (12, 24)
+PASS_COLUMNS = 512
 LAG = 2
 LEAD = 4
 EARLY = 1
@@ -85,21 +86,24 @@ def tile_rnadeoutputlayer_kernel(
             d_scalar = d_vector + d_tensor
             if d_tensor > 0:
                 bank = psum_tp.tile([P, d_tensor, rows * PACK], BF16, tag="tp")
-                nc.tensor.matmul(
-                    out=bank[:].rearrange("p d m -> p m d"),
-                    lhsT=ident_bf[:],
-                    rhs=raw_mj[:, :, d_vector:d_scalar],
-                    start=True,
-                    stop=True,
-                )
-            for copy, d_range in (
-                (nc.vector.tensor_copy, slice(0, d_vector)),
-                (nc.scalar.copy, slice(d_scalar, D)),
-            ):
-                copy(
-                    out=tile[:, d_range, cols].rearrange("p (c i) m -> p c m i", i=RUN),
-                    in_=raw_mj[:, :, d_range].rearrange("p m (c i) -> p c m i", i=RUN),
-                )
+                width = PASS_COLUMNS // (rows * PACK)
+                for first_d in range(0, d_tensor, width):
+                    last_d = min(first_d + width, d_tensor)
+                    nc.tensor.matmul(
+                        out=bank[:, first_d:last_d, :].rearrange("p d m -> p m d"),
+                        lhsT=ident_bf[:],
+                        rhs=raw_mj[:, :, d_vector + first_d : d_vector + last_d],
+                        start=True,
+                        stop=True,
+                    )
+            nc.vector.tensor_copy(
+                out=tile[:, 0:d_vector, cols].rearrange("p (c i) (m j) -> p c m i j", i=RUN, j=2),
+                in_=raw_mj[:, :, 0:d_vector].rearrange("p (m j) (c i) -> p c m i j", i=RUN, j=2),
+            )
+            nc.scalar.copy(
+                out=tile[:, d_scalar:D, cols].rearrange("p (c i) m -> p c m i", i=RUN),
+                in_=raw_mj[:, :, d_scalar:D].rearrange("p m (c i) -> p c m i", i=RUN),
+            )
             if d_tensor > 0:
                 nc.scalar.copy(out=tile[:, d_vector:d_scalar, cols], in_=bank[:])
 
@@ -339,15 +343,15 @@ def tile_rnadeoutputlayer_kernel(
                         clip(g - 2)
 
             for c in range(CHUNKS):
-                regroup(V_mu, c * CHUNK, CHUNK, grouped, D_VECTOR_MU, D_TENSOR_MU)
+                regroup(V_mu, c * CHUNK, CHUNK, grouped, D_VECTOR_MU[0], D_TENSOR_MU[0])
                 if c < LAG:
                     exp_and_sum(CHUNKS - LAG + c, 0, by_b_of[CHUNKS - LAG + c])
                 if c >= LEAD:
                     sigma_pair(c - LEAD)
             for n in range(CHUNKS - LEAD, CHUNKS):
                 sigma_pair(n)
-            quantise(range(D_VECTOR_MU, D), 0, grouped, w_codes, w_scales)
-            quantise(range(0, D_VECTOR_MU), 0, grouped, w_codes, w_scales)
+            quantise(range(D_VECTOR_MU[1], D), 0, grouped, w_codes, w_scales)
+            quantise(range(0, D_VECTOR_MU[1]), 0, grouped, w_codes, w_scales)
             clip(N_GROUPS - 2)
             clip(N_GROUPS - 1)
             for g in range(AHEAD):
@@ -355,7 +359,7 @@ def tile_rnadeoutputlayer_kernel(
             for c in range(CHUNKS):
                 g = CHUNKS + c
                 by_b_of[g] = turn(lambda i: [neg_a[:, g * GROUP + i, :]])
-                regroup(V_mu, HALF + c * CHUNK, CHUNK, grouped, D_VECTOR_MU, D_TENSOR_MU)
+                regroup(V_mu, HALF + c * CHUNK, CHUNK, grouped, D_VECTOR_MU[1], D_TENSOR_MU[1])
                 minimum(g, 0, by_b_of[g])
                 if c >= LAG:
                     exp_and_sum(g - LAG, 0, by_b_of[g - LAG])

import math

import concourse.mybir as mybir
from concourse.masks import make_identity

BF16 = mybir.dt.bfloat16
F32 = mybir.dt.float32
U32 = mybir.dt.uint32
U8 = mybir.dt.uint8
FP8X4 = mybir.dt.float8_e4m3fn_x4
ALU = mybir.AluOpType
ACT = mybir.ActivationFunctionType
AX = mybir.AxisListType

P = 128
ROWS = 128
H = 512
D = 64
PACK = 4
HALF = 64
CHUNK = 8
CHUNKS = HALF // CHUNK
SHARE = D // CHUNKS
RUN = 4
D_VECTOR_FIRST = (32, 24)
D_VECTOR_SIGMA = (40, 48)
D_VECTOR_MU = (40, 32)
D_TENSOR_MU = (12, 24)
PASS_COLUMNS = 512
LAG = 2
LEAD = 4
EARLY = 1
AHEAD = 2
GROUP = 4
N_GROUPS = D // GROUP
Y_BANK = 8
HALF_LOG_2PI = 0.5 * math.log(2.0 * math.pi)

FLOPS = 2 * ROWS * ROWS * H * D * 3


def tile_rnadeoutputlayer_kernel(
    tc, x, input_var, V_alpha, V_mu, V_sigma, b_alpha, b_mu, b_sigma, out
):
    nc = tc.nc
    engines = mybir.EngineType
    with (
        tc.tile_pool(name="keep", bufs=1) as keep,
        tc.tile_pool(name="raw", bufs=7) as raw_pool,
        tc.tile_pool(name="work", bufs=2) as work,
        tc.psum_pool(name="acc", bufs=3) as psum_acc,
        tc.psum_pool(name="tp", bufs=5) as psum_tp,
    ):
        ident = keep.tile([P, P], F32)
        make_identity(nc, ident[:])
        ident_bf = keep.tile([P, P], BF16)
        make_identity(nc, ident_bf[:])

        y_bf = keep.tile([P, D], BF16)
        nc.scalar.dma_start(out=y_bf[:], in_=input_var)
        bias_bf = keep.tile([P, 3, D], BF16)
        nc.scalar.dma_start(out=bias_bf[:, 0, :], in_=b_sigma)
        nc.scalar.dma_start(out=bias_bf[:, 1, :], in_=b_mu)
        nc.scalar.dma_start(out=bias_bf[:, 2, :], in_=b_alpha)
        bias_sigma = keep.tile([P, D], F32)
        bias_mu = keep.tile([P, D], F32)
        neg_bias_alpha = keep.tile([P, D], F32)

        grouped = keep.tile([P, D, HALF * PACK], BF16, align_bytes=64)
        x_codes = keep.tile([P, D, ROWS], U32, align_bytes=64)
        x_scales = keep.tile([P, D, ROWS], U8, align_bytes=64)
        w_codes = keep.tile([P, D, ROWS], U32, align_bytes=64)
        w_scales = keep.tile([P, D, ROWS], U8, align_bytes=64)
        neg_a = keep.tile([P, D, ROWS], F32)
        y_all = keep.tile([P, D, ROWS], BF16)
        neg_max = keep.tile([P, 2, D], F32)
        exp_sum = keep.tile([P, 2, D], F32)

        def regroup(src, first_row, rows, tile, d_vector, d_tensor=0):
            by_partition = src.rearrange("r (p j) d -> p r (j d)", j=PACK)
            raw = raw_pool.tile([P, rows, PACK * D], BF16, tag="raw")
            nc.sync.dma_start(out=raw[:], in_=by_partition[:, first_row : first_row + rows, :])
            raw_mj = raw[:].rearrange("p r (j d) -> p (r j) d", j=PACK)
            first = first_row % HALF
            cols = slice(first * PACK, (first + rows) * PACK)
            d_scalar = d_vector + d_tensor
            if d_tensor > 0:
                bank = psum_tp.tile([P, d_tensor, rows * PACK], BF16, tag="tp")
                width = PASS_COLUMNS // (rows * PACK)
                for first_d in range(0, d_tensor, width):
                    last_d = min(first_d + width, d_tensor)
                    nc.tensor.matmul(
                        out=bank[:, first_d:last_d, :].rearrange("p d m -> p m d"),
                        lhsT=ident_bf[:],
                        rhs=raw_mj[:, :, d_vector + first_d : d_vector + last_d],
                        start=True,
                        stop=True,
                    )
            nc.vector.tensor_copy(
                out=tile[:, 0:d_vector, cols].rearrange("p (c i) (m j) -> p c m i j", i=RUN, j=2),
                in_=raw_mj[:, :, 0:d_vector].rearrange("p (m j) (c i) -> p c m i j", i=RUN, j=2),
            )
            nc.scalar.copy(
                out=tile[:, d_scalar:D, cols].rearrange("p (c i) m -> p c m i", i=RUN),
                in_=raw_mj[:, :, d_scalar:D].rearrange("p m (c i) -> p c m i", i=RUN),
            )
            if d_tensor > 0:
                nc.scalar.copy(out=tile[:, d_vector:d_scalar, cols], in_=bank[:])

        def quantise(ds, half, tile, codes, scales):
            rows = slice(half * HALF, (half + 1) * HALF)
            for d in ds:
                nc.vector.quantize_mx(
                    out=codes[:, d, rows].bitcast(FP8X4),
                    scales=scales[:, d, rows],
                    in_=tile[:, d, :],
                )

        def share(c):
            return range(c * SHARE, (c + 1) * SHARE)

        def extra_pass(acc):
            nc.tensor.matmul_mx(
                out=acc[:].rearrange("p d b -> p (d b)"),
                lhsT=x_codes[:, 0, :].bitcast(FP8X4),
                lhsT_scale=x_scales[:, 0, :],
                rhs=x_codes[:, 0:GROUP, :].rearrange("p d r -> p (d r)").bitcast(FP8X4),
                rhs_scale=x_scales[:, 0:GROUP, :].rearrange("p d r -> p (d r)"),
                start=True,
                stop=True,
            )

        def products(g, extra=False):
            acc = psum_acc.tile([P, GROUP, ROWS], F32, tag="acc")
            if extra:
                extra_pass(acc)
            for i in range(GROUP):
                d = g * GROUP + i
                nc.tensor.matmul_mx(
                    out=acc[:, i, :],
                    lhsT=w_codes[:, d, :].bitcast(FP8X4),
                    lhsT_scale=w_scales[:, d, :],
                    rhs=x_codes[:, d, :].bitcast(FP8X4),
                    rhs_scale=x_scales[:, d, :],
                    start=True,
                    stop=True,
                )
            return acc

        def add_bias(g, acc, target, bias, scale):
            for i in range(GROUP):
                d = g * GROUP + i
                nc.scalar.activation(
                    out=target[:, d, :],
                    in_=acc[:, i, :],
                    func=ACT.Identity,
                    bias=bias[:, d : d + 1],
                    scale=scale,
                )

        def turn(terms_of):
            by_b = psum_tp.tile([P, GROUP, ROWS], F32, tag="tp")
            for i in range(GROUP):
                terms = terms_of(i)
                for t, term in enumerate(terms):
                    nc.tensor.matmul(
                        out=by_b[:, i, :],
                        lhsT=term,
                        rhs=ident[:],
                        is_transpose=True,
                        start=(t == 0),
                        stop=(t == len(terms) - 1),
                    )
            return by_b

        def minimum(g, w, by_b):
            ds = slice(g * GROUP, (g + 1) * GROUP)
            nc.vector.tensor_reduce(out=neg_max[:, w, ds], in_=by_b[:], axis=AX.X, op=ALU.min)

        def exp_and_sum(g, w, by_b):
            unused = work.tile([P, GROUP, ROWS], BF16, tag="unused")
            for i in range(GROUP):
                d = g * GROUP + i
                nc.scalar.activation(
                    out=unused[:, i, :],
                    in_=by_b[:, i, :],
                    func=ACT.Exp,
                    bias=neg_max[:, w, d : d + 1],
                    scale=-1.0,
                    accum_out=exp_sum[:, w, d : d + 1],
                )

        def spread_y(first):
            bank = psum_acc.tile([P, Y_BANK, ROWS], BF16, tag="acc")
            for i in range(Y_BANK):
                d = first + i
                nc.tensor.matmul(
                    out=bank[:, i, :],
                    lhsT=y_bf[:, d : d + 1].to_broadcast([P, P]),
                    rhs=ident_bf[:],
                    is_transpose=True,
                    start=True,
                    stop=True,
                )
            nc.vector.tensor_copy(out=y_all[:, first : first + Y_BANK, :], in_=bank[:])

        ordered = {engines.PE, engines.DVE, engines.Activation, engines.Pool}
        with tc.tile_pool(name="early", bufs=1) as early, tc.manual_schedule(engines=ordered):
            grouped_too = early.tile([P, D, HALF * PACK], BF16, align_bytes=64)
            acc_of = {}

            for first_row, rows in ((0, 2), (2, 2), (4, 4)):
                regroup(x, first_row, rows, grouped, D_VECTOR_FIRST[0])
            for c in range(1, CHUNKS):
                regroup(x, c * CHUNK, CHUNK, grouped, D_VECTOR_FIRST[c % 2])
                spread_y((c - 1) * Y_BANK)
            for c in range(CHUNKS):
                regroup(x, HALF + c * CHUNK, CHUNK, grouped_too, D_VECTOR_FIRST[c % 2])
                quantise(share(c), 0, grouped, x_codes, x_scales)
            spread_y((CHUNKS - 1) * Y_BANK)
            nc.vector.tensor_copy(out=bias_sigma[:], in_=bias_bf[:, 0, :])
            nc.vector.tensor_copy(out=bias_mu[:], in_=bias_bf[:, 1, :])
            nc.vector.tensor_scalar(
                out=neg_bias_alpha[:],
                in0=bias_bf[:, 2, :],
                scalar1=-1.0,
                scalar2=None,
                op0=ALU.mult,
            )

            for c in range(CHUNKS):
                regroup(V_alpha, c * CHUNK, CHUNK, grouped, D_VECTOR_FIRST[c % 2])
                quantise(share(c), 1, grouped_too, x_codes, x_scales)
            for c in range(CHUNKS):
                regroup(V_alpha, HALF + c * CHUNK, CHUNK, grouped_too, D_VECTOR_FIRST[c % 2])
                quantise(share(c), 0, grouped, w_codes, w_scales)

            for c in range(CHUNKS):
                regroup(V_sigma, c * CHUNK, CHUNK, grouped, D_VECTOR_SIGMA[c % 2])
                quantise(share(c), 1, grouped_too, w_codes, w_scales)
                for g in (2 * c, 2 * c + 1):
                    add_bias(g, products(g), neg_a, neg_bias_alpha, -1.0)
            by_b_of = {}
            for c in range(CHUNKS):
                by_b_of[c] = turn(lambda i: [neg_a[:, c * GROUP + i, :]])
                regroup(V_sigma, HALF + c * CHUNK, CHUNK, grouped_too, D_VECTOR_SIGMA[c % 2])
                quantise(share(c), 0, grouped, w_codes, w_scales)
                if c >= LAG:
                    minimum(c - LAG, 0, by_b_of[c - LAG])
                    exp_and_sum(c - LAG, 0, by_b_of[c - LAG])
            for g in range(CHUNKS - LAG, CHUNKS):
                minimum(g, 0, by_b_of[g])
            for g in range(N_GROUPS):
                quantise(range(g * GROUP, (g + 1) * GROUP), 1, grouped_too, w_codes, w_scales)

        with tc.tile_pool(name="late", bufs=1) as late, tc.manual_schedule(engines=ordered):
            log_sigma = late.tile([P, D, ROWS], F32)
            half_z2_of = {}
            inv_sigma_of = {}

            def clip(g):
                ds = slice(g * GROUP, (g + 1) * GROUP)
                nc.vector.tensor_scalar(
                    out=log_sigma[:, ds, :],
                    in0=log_sigma[:, ds, :],
                    scalar1=-20.0,
                    scalar2=20.0,
                    op0=ALU.max,
                    op1=ALU.min,
                )

            def passes(g):
                acc_of[g] = products(g, True)

            def invert(g):
                ds = slice(g * GROUP, (g + 1) * GROUP)
                inv_sigma = work.tile([P, GROUP, ROWS], F32, tag="inv_sigma", bufs=AHEAD + 1)
                nc.scalar.activation(
                    out=inv_sigma[:],
                    in_=log_sigma[:, ds, :],
                    func=ACT.Exp,
                    bias=-0.5 * math.log(2.0),
                    scale=-1.0,
                )
                inv_sigma_of[g] = inv_sigma

            def difference(g):
                acc = acc_of[g]
                half_z2 = work.tile([P, GROUP, ROWS], F32, tag="half_z2", bufs=3)
                for i in range(GROUP):
                    d = g * GROUP + i
                    nc.vector.scalar_tensor_tensor(
                        out=half_z2[:, i, :],
                        in0=acc[:, i, :],
                        scalar=bias_mu[:, d : d + 1],
                        in1=y_all[:, d, :],
                        op0=ALU.add,
                        op1=ALU.subtract,
                    )
                half_z2_of[g] = half_z2

            def scale(g):
                half_z2 = half_z2_of[g]
                engine = nc.vector if g % 4 == 3 else nc.gpsimd
                engine.tensor_tensor(
                    out=half_z2[:], in0=half_z2[:], in1=inv_sigma_of[g][:], op=ALU.mult
                )
                if g % 4 == 3 and g < N_GROUPS - 1:
                    nc.gpsimd.tensor_tensor(
                        out=half_z2[:], in0=half_z2[:], in1=half_z2[:], op=ALU.mult
                    )

            def square(g):
                half_z2 = half_z2_of[g]
                if g % 4 != 3 or g == N_GROUPS - 1:
                    nc.scalar.activation(out=half_z2[:], in_=half_z2[:], func=ACT.Square)

            def flip(by_b, i, term, start, stop):
                nc.tensor.matmul(
                    out=by_b[:, i, :],
                    lhsT=term,
                    rhs=ident[:],
                    is_transpose=True,
                    start=start,
                    stop=stop,
                )

            def begin_exponent(g):
                by_b = psum_tp.tile([P, GROUP, ROWS], F32, tag="tp")
                for i in range(GROUP):
                    flip(by_b, i, neg_a[:, g * GROUP + i, :], i == 0, False)
                    flip(by_b, i, log_sigma[:, g * GROUP + i, :], False, False)
                by_b_of[g] = by_b

            def end_exponent(g):
                for i in range(GROUP):
                    flip(by_b_of[g], i, half_z2_of[g][:, i, :], False, i == GROUP - 1)

            def sigma_pair(n):
                for g in (2 * n, 2 * n + 1):
                    add_bias(g, products(g), log_sigma, bias_sigma, 1.0)
                    if g >= 2:
                        clip(g - 2)

            for c in range(CHUNKS):
                regroup(V_mu, c * CHUNK, CHUNK, grouped, D_VECTOR_MU[0], D_TENSOR_MU[0])
                if c < LAG:
                    exp_and_sum(CHUNKS - LAG + c, 0, by_b_of[CHUNKS - LAG + c])
                if c >= LEAD:
                    sigma_pair(c - LEAD)
            for n in range(CHUNKS - LEAD, CHUNKS):
                sigma_pair(n)
            quantise(range(D_VECTOR_MU[1], D), 0, grouped, w_codes, w_scales)
            quantise(range(0, D_VECTOR_MU[1]), 0, grouped, w_codes, w_scales)
            clip(N_GROUPS - 2)
            clip(N_GROUPS - 1)
            for g in range(AHEAD):
                invert(g)
            for c in range(CHUNKS):
                g = CHUNKS + c
                by_b_of[g] = turn(lambda i: [neg_a[:, g * GROUP + i, :]])
                regroup(V_mu, HALF + c * CHUNK, CHUNK, grouped, D_VECTOR_MU[1], D_TENSOR_MU[1])
                minimum(g, 0, by_b_of[g])
                if c >= LAG:
                    exp_and_sum(g - LAG, 0, by_b_of[g - LAG])
            for g in range(N_GROUPS - LAG, N_GROUPS):
                exp_and_sum(g, 0, by_b_of[g])

            def quantise_rest(g):
                quantise(range(g * GROUP, (g + 1) * GROUP), 1, grouped, w_codes, w_scales)

            for g in range(EARLY):
                begin_exponent(g)
            quantise_rest(0)
            quantise_rest(1)
            passes(0)
            for s in range(N_GROUPS + 2):
                if s < N_GROUPS:
                    difference(s)
                    scale(s)
                if 1 <= s <= N_GROUPS:
                    square(s - 1)
                if s + 1 < N_GROUPS:
                    passes(s + 1)
                if s + AHEAD < N_GROUPS:
                    invert(s + AHEAD)
                if s + 2 < N_GROUPS:
                    quantise_rest(s + 2)
                if N_GROUPS - 2 <= s < N_GROUPS:
                    extra_pass(psum_acc.tile([P, GROUP, ROWS], F32, tag="acc", name="unread"))
                if s == N_GROUPS:
                    extra_pass(psum_acc.tile([P, GROUP, ROWS], F32, tag="acc", name="unread"))
                    extra_pass(psum_acc.tile([P, GROUP, ROWS], F32, tag="acc", name="unread"))
                if 1 <= s <= N_GROUPS:
                    end_exponent(s - 1)
                if s + EARLY < N_GROUPS:
                    begin_exponent(s + EARLY)
                if s >= 2:
                    minimum(s - 2, 1, by_b_of[s - 2])
                    exp_and_sum(s - 2, 1, by_b_of[s - 2])

            max_part = late.tile([P, D], F32)
            nc.vector.tensor_tensor(
                out=max_part[:], in0=neg_max[:, 0, :], in1=neg_max[:, 1, :], op=ALU.subtract
            )
            max_total = late.tile([P, 1], F32)
            nc.vector.tensor_reduce(out=max_total[:], in_=max_part[:], axis=AX.X, op=ALU.add)
            constant = late.tile([P, 1], F32)
            nc.vector.tensor_scalar(
                out=constant[:],
                in0=max_total[:],
                scalar1=-D * HALF_LOG_2PI,
                scalar2=None,
                op0=ALU.add,
            )
            log_sum = late.tile([P, 2, D], F32)
            log_total = late.tile([P, 2], F32)
            for w in range(2):
                nc.scalar.activation(
                    out=log_sum[:, w, :],
                    in_=exp_sum[:, w, :],
                    func=ACT.Ln,
                    accum_out=log_total[:, w : w + 1],
                )
            repeated = work.tile([P, P], F32, tag="half_z2", bufs=3)
            nc.vector.tensor_scalar(
                out=repeated[:],
                in0=log_total[:, 1:2].to_broadcast([P, P]),
                scalar1=log_total[:, 0:1],
                scalar2=constant[:],
                op0=ALU.subtract,
                op1=ALU.add,
            )
            as_row = psum_tp.tile([P, P], F32, tag="tp")
            nc.tensor.transpose(as_row[:], repeated[:], ident[:])
            row = work.tile([P, P], F32, tag="half_z2", bufs=3)
            nc.vector.tensor_copy(out=row[:], in_=as_row[:])
            nc.sync.dma_start(out=out.rearrange("(o b) -> o b", o=1), in_=row[0:1, :])
